import numpy as np
import ml_dtypes


def mxq(x, axis, fmt="e4m3"):
    dtype, down = {"e4m3": (ml_dtypes.float8_e4m3fn, 7), "e5m2": (ml_dtypes.float8_e5m2, 14)}[fmt]
    v = np.moveaxis(np.asarray(x, np.float32).astype(ml_dtypes.bfloat16).astype(np.float64), axis, -1)
    blocks = v.reshape(v.shape[:-1] + (-1, 32))
    amax = np.abs(blocks).max(-1, keepdims=True)
    byte = np.maximum(np.where(amax > 0, np.frexp(amax)[1] - 1 + 127, 0) - down, 1)
    scale = np.exp2(byte - 127.0)
    codes = (blocks / scale).astype(np.float32).astype(dtype).astype(np.float64)
    return np.moveaxis((codes * scale).reshape(v.shape), -1, axis)


WIDE = False


def mx_kscale(k):
    if not WIDE:
        return np.ones(k)
    levels = np.array([10, -10, 5, -5, 0])
    a = np.random.permutation(np.resize(levels, k // 512 * 4)).reshape(k // 512, 4)
    idx = np.arange(k)
    return np.exp2(a[idx // 512, idx % 128 // 32])


BF16 = ml_dtypes.bfloat16


def bf(x):
    return np.asarray(x, np.float32).astype(BF16)


def f64(x):
    return np.asarray(x).astype(np.float64)


B, HH, WW, E, NH, D = 1, 512, 4, 1024, 8, 128
KD = NH * D


def setup_inputs():
    t = mx_kscale(KD)
    return {"ret_w": bf(np.random.standard_normal((B, HH, WW, NH, D)) * 0.9),
            "kv_h": bf(np.random.standard_normal((B, WW, NH, D, D)) * 0.8 * t.reshape(NH, 1, D)),
            "Wo": bf(np.random.standard_normal((E, KD)) * 0.3 / np.sqrt(KD) / t),
            "bo": bf(np.random.standard_normal(E) * 0.2)}


def reference(ret_w, kv_h, Wo, bo):
    o = f64(ret_w).reshape(B, HH, WW * NH, D).transpose(0, 2, 1, 3) @ f64(kv_h).reshape(B, WW * NH, D, D)
    o = o.transpose(0, 2, 1, 3).reshape(B, HH, WW, KD)
    y = (mxq(o, 3, "e4m3") @ mxq(f64(Wo).T, 0, "e4m3")) + f64(bo)
    return y.reshape(B, HH * WW, E)

@@ -1,0 +1,170 @@
+from contextlib import ExitStack
+
+import concourse.mybir as mybir
+from concourse.masks import make_identity
+
+BF16 = mybir.dt.bfloat16
+F32 = mybir.dt.float32
+U32 = mybir.dt.uint32
+U8 = mybir.dt.uint8
+FP8X4 = mybir.dt.float8_e4m3fn_x4
+
+P = 128
+HEIGHT, WIDTH, HEADS, HEAD_DIM, OUT_CH = 512, 4, 8, 128, 1024
+CHANNELS = HEADS * HEAD_DIM
+PACK = 4
+PASSES = CHANNELS // (P * PACK)
+UNITS = (HEIGHT // P) * WIDTH
+N_TILE = 512
+COL_HALVES = OUT_CH // N_TILE
+WO_PER_ROUND = 2
+WO_ROUNDS = OUT_CH // P // WO_PER_ROUND
+WO_COLS = WO_PER_ROUND * P
+MX_LAG = WO_ROUNDS
+
+FLOPS = 2 * HEIGHT * WIDTH * CHANNELS * HEAD_DIM + 2 * HEIGHT * WIDTH * CHANNELS * OUT_CH
+
+
+def tile_linear_retention_pb_kernel(tc, ret_w, kv_h, Wo, bo, out):
+    nc = tc.nc
+
+    x_dram = ret_w[0].rearrange("(hb h) w n e -> hb w h (n e)", h=P)
+    kv_dram = kv_h[0].rearrange("w n e f -> w e n f")
+    wo_dram = Wo.rearrange("(cb c) k -> c cb k", c=P)
+    out_dram = out[0].rearrange("(hb h w) c -> hb w h c", h=P, w=WIDTH)
+
+    with ExitStack() as ctx:
+        keep = ctx.enter_context(tc.tile_pool(name="keep", bufs=1))
+        work = ctx.enter_context(tc.tile_pool(name="work", bufs=3))
+        quantised = ctx.enter_context(tc.tile_pool(name="quantised", bufs=MX_LAG))
+        results = ctx.enter_context(tc.tile_pool(name="results", bufs=6))
+        psum_t = ctx.enter_context(tc.psum_pool(name="psum_t", bufs=3))
+        psum_o = ctx.enter_context(tc.psum_pool(name="psum_o", bufs=3))
+        psum_y = ctx.enter_context(tc.psum_pool(name="psum_y", bufs=2))
+        ctx.enter_context(tc.manual_schedule())
+
+        x_sb = keep.tile([P, UNITS, CHANNELS], BF16)
+        kv_sb = keep.tile([P, WIDTH * HEADS, HEAD_DIM], BF16)
+        wo_sb = keep.tile([P, OUT_CH // P, CHANNELS], BF16)
+        for u in range(UNITS):
+            if u < WO_ROUNDS:
+                blocks = slice(u * WO_PER_ROUND, (u + 1) * WO_PER_ROUND)
+                nc.sync.dma_start(out=wo_sb[:, blocks, :], in_=wo_dram[:, blocks, :])
+            nc.sync.dma_start(out=x_sb[:, u, :], in_=x_dram[u // WIDTH, u % WIDTH])
+            if u < WIDTH:
+                nc.sync.dma_start(out=kv_sb[:, u * HEADS : (u + 1) * HEADS, :], in_=kv_dram[u])
+
+        ident = keep.tile([P, P], BF16)
+        make_identity(nc, ident[:])
+
+        ones = keep.tile([P, P], BF16)
+        nc.vector.memset(ones[:], 1.0)
+        bias_rows = keep.tile([P, OUT_CH], BF16)
+        nc.vector.memset(bias_rows[:], 0.0)
+        nc.scalar.dma_start(out=bias_rows[0:1, :], in_=bo.rearrange("(o c) -> o c", o=1))
+        bias = keep.tile([P, OUT_CH], F32)
+        for ch in range(COL_HALVES):
+            cols = slice(ch * N_TILE, (ch + 1) * N_TILE)
+            spread = psum_y.tile([P, N_TILE], F32, tag="y_ps")
+            nc.tensor.matmul(out=spread[:], lhsT=ones[:], rhs=bias_rows[:, cols], start=True, stop=True)
+            nc.vector.tensor_copy(out=bias[:, cols], in_=spread[:])
+
+        wo_grouped = keep.tile([P, PASSES, OUT_CH, PACK], BF16, align_bytes=64)
+        wo_codes = keep.tile([P, PASSES, OUT_CH], U32, align_bytes=64)
+        wo_scales = keep.tile([P, PASSES, OUT_CH], U8, align_bytes=64)
+
+        def transpose_wo_block(cb):
+            wo_t = psum_t.tile([P, HEADS, P], BF16, tag="t_ps")
+            for n in range(HEADS):
+                nc.tensor.transpose(
+                    out=wo_t[:, n, :], in_=wo_sb[:, cb, n * P : (n + 1) * P], identity=ident[:]
+                )
+            nc.vector.tensor_copy(
+                out=wo_grouped[:, :, cb * P : (cb + 1) * P, :],
+                in_=wo_t[:].rearrange("p (g t) c -> p g c t", t=PACK),
+            )
+
+        def quantise_wo(j):
+            cols = slice(j * WO_COLS, (j + 1) * WO_COLS)
+            for g in range(PASSES):
+                nc.vector.quantize_mx(
+                    out=wo_codes[:, g, cols].bitcast(FP8X4),
+                    scales=wo_scales[:, g, cols],
+                    in_=wo_grouped[:, g, cols, :].rearrange("p c t -> p (c t)"),
+                )
+
+        x_t = {}
+        o_grouped = {}
+        o_codes = {}
+        o_scales = {}
+
+        def transpose_unit(u):
+            x_t_ps = psum_t.tile([P, HEADS, P], BF16, tag="t_ps")
+            for n in range(HEADS):
+                nc.tensor.transpose(
+                    out=x_t_ps[:, n, :], in_=x_sb[:, u, n * P : (n + 1) * P], identity=ident[:]
+                )
+            x_t_sb = work.tile([P, HEADS, P], BF16, tag="x_t")
+            nc.scalar.copy(out=x_t_sb[:], in_=x_t_ps[:])
+            x_t[u] = x_t_sb
+
+        def read_out(u):
+            w = u % WIDTH
+            grouped = work.tile([P, PASSES, P, PACK], BF16, tag="o_grouped", align_bytes=64)
+            for g in range(PASSES):
+                o_ps = psum_o.tile([P, PACK, P], F32, tag="o_ps")
+                for t in range(PACK):
+                    n = g * PACK + t
+                    nc.tensor.matmul(
+                        out=o_ps[:, t, :],
+                        lhsT=kv_sb[:, w * HEADS + n, :],
+                        rhs=x_t[u][:, n, :],
+                        start=True,
+                        stop=True,
+                    )
+                nc.scalar.copy(out=grouped[:, g], in_=o_ps[:].rearrange("p t h -> p h t"))
+            o_grouped[u] = grouped
+
+        def quantise_unit(u):
+            codes = quantised.tile([P, PASSES, P], U32, tag="o_codes", align_bytes=64)
+            scales = quantised.tile([P, PASSES, P], U8, tag="o_scales", align_bytes=64)
+            nc.vector.quantize_mx(
+                out=codes[:].rearrange("p g h -> p (g h)").bitcast(FP8X4),
+                scales=scales[:].rearrange("p g h -> p (g h)"),
+                in_=o_grouped[u][:].rearrange("p g h t -> p (g h t)"),
+            )
+            o_codes[u] = codes
+            o_scales[u] = scales
+
+        def project(u):
+            for ch in range(COL_HALVES):
+                cols = slice(ch * N_TILE, (ch + 1) * N_TILE)
+                y_ps = psum_y.tile([P, N_TILE], F32, tag="y_ps")
+                for g in range(PASSES):
+                    nc.tensor.matmul_mx(
+                        out=y_ps[:],
+                        lhsT=o_codes[u][:, g, :].bitcast(FP8X4),
+                        lhsT_scale=o_scales[u][:, g, :],
+                        rhs=wo_codes[:, g, cols].bitcast(FP8X4),
+                        rhs_scale=wo_scales[:, g, cols],
+                        start=(g == 0),
+                        stop=(g == PASSES - 1),
+                    )
+                y = results.tile([P, N_TILE], F32, tag="y")
+                nc.vector.tensor_tensor(out=y[:], in0=y_ps[:], in1=bias[:, cols], op=mybir.AluOpType.add)
+                nc.sync.dma_start(out=out_dram[u // WIDTH, u % WIDTH][:, cols], in_=y[:])
+
+        for i in range(UNITS + MX_LAG):
+            if i < WO_ROUNDS:
+                for cb in range(i * WO_PER_ROUND, (i + 1) * WO_PER_ROUND):
+                    transpose_wo_block(cb)
+            if i < UNITS:
+                transpose_unit(i)
+            if 0 <= i - 1 < UNITS:
+                read_out(i - 1)
+            if 0 <= i - 2 < UNITS:
+                quantise_unit(i - 2)
+            if 0 <= i - 1 < WO_ROUNDS:
+                quantise_wo(i - 1)
+            if 0 <= i - MX_LAG:
+                project(i - MX_LAG)

@@ -14,13 +14,15 @@ HEIGHT, WIDTH, HEADS, HEAD_DIM, OUT_CH = 512, 4, 8, 128, 1024
 CHANNELS = HEADS * HEAD_DIM
 PACK = 4
 PASSES = CHANNELS // (P * PACK)
-UNITS = (HEIGHT // P) * WIDTH
+H_BLOCKS = HEIGHT // P
+UNITS = WIDTH * H_BLOCKS
 N_TILE = 512
 COL_HALVES = OUT_CH // N_TILE
-WO_PER_ROUND = 2
-WO_ROUNDS = OUT_CH // P // WO_PER_ROUND
-WO_COLS = WO_PER_ROUND * P
-MX_LAG = WO_ROUNDS
+WO_BLOCKS = OUT_CH // P
+MX_UNITS = 2
+ROUNDS = UNITS + 2
+MX_FIRST = ROUNDS - UNITS // MX_UNITS
+assert MX_FIRST > WO_BLOCKS + 1
 
 FLOPS = 2 * HEIGHT * WIDTH * CHANNELS * HEAD_DIM + 2 * HEIGHT * WIDTH * CHANNELS * OUT_CH
 
@@ -28,46 +30,49 @@ FLOPS = 2 * HEIGHT * WIDTH * CHANNELS * HEAD_DIM + 2 * HEIGHT * WIDTH * CHANNELS
 def tile_linear_retention_pb_kernel(tc, ret_w, kv_h, Wo, bo, out):
     nc = tc.nc
 
-    x_dram = ret_w[0].rearrange("(hb h) w n e -> hb w h (n e)", h=P)
+    x_dram = ret_w[0].rearrange("(hb h) w n e -> w hb h (n e)", h=P)
     kv_dram = kv_h[0].rearrange("w n e f -> w e n f")
     wo_dram = Wo.rearrange("(cb c) k -> c cb k", c=P)
-    out_dram = out[0].rearrange("(hb h w) c -> hb w h c", h=P, w=WIDTH)
+    out_dram = out[0].rearrange("(hb h w) c -> w hb h c", h=P, w=WIDTH)
 
     with ExitStack() as ctx:
         keep = ctx.enter_context(tc.tile_pool(name="keep", bufs=1))
         work = ctx.enter_context(tc.tile_pool(name="work", bufs=3))
-        quantised = ctx.enter_context(tc.tile_pool(name="quantised", bufs=MX_LAG))
-        results = ctx.enter_context(tc.tile_pool(name="results", bufs=6))
-        psum_t = ctx.enter_context(tc.psum_pool(name="psum_t", bufs=3))
-        psum_o = ctx.enter_context(tc.psum_pool(name="psum_o", bufs=3))
-        psum_y = ctx.enter_context(tc.psum_pool(name="psum_y", bufs=2))
+        quantised = ctx.enter_context(tc.tile_pool(name="quantised", bufs=MX_FIRST))
+        results = ctx.enter_context(tc.tile_pool(name="results", bufs=8))
+        psum_t = ctx.enter_context(tc.psum_pool(name="psum_t", bufs=2))
+        psum_o = ctx.enter_context(tc.psum_pool(name="psum_o", bufs=PASSES))
+        psum_y = ctx.enter_context(tc.psum_pool(name="psum_y", bufs=MX_UNITS * COL_HALVES))
         ctx.enter_context(tc.manual_schedule())
 
-        x_sb = keep.tile([P, UNITS, CHANNELS], BF16)
-        kv_sb = keep.tile([P, WIDTH * HEADS, HEAD_DIM], BF16)
-        wo_sb = keep.tile([P, OUT_CH // P, CHANNELS], BF16)
-        for u in range(UNITS):
-            if u < WO_ROUNDS:
-                blocks = slice(u * WO_PER_ROUND, (u + 1) * WO_PER_ROUND)
-                nc.sync.dma_start(out=wo_sb[:, blocks, :], in_=wo_dram[:, blocks, :])
-            nc.sync.dma_start(out=x_sb[:, u, :], in_=x_dram[u // WIDTH, u % WIDTH])
-            if u < WIDTH:
-                nc.sync.dma_start(out=kv_sb[:, u * HEADS : (u + 1) * HEADS, :], in_=kv_dram[u])
-
+        bias_rows = keep.tile([P, OUT_CH], BF16)
+        nc.vector.memset(bias_rows[:], 0.0)
+        ones = keep.tile([P, P], BF16)
+        nc.vector.memset(ones[:], 1.0)
         ident = keep.tile([P, P], BF16)
         make_identity(nc, ident[:])
 
-        ones = keep.tile([P, P], BF16)
-        nc.vector.memset(ones[:], 1.0)
-        bias_rows = keep.tile([P, OUT_CH], BF16)
-        nc.vector.memset(bias_rows[:], 0.0)
-        nc.scalar.dma_start(out=bias_rows[0:1, :], in_=bo.rearrange("(o c) -> o c", o=1))
+        x_sb = keep.tile([P, UNITS, CHANNELS], BF16)
+        kv_sb = keep.tile([P, WIDTH, HEADS, HEAD_DIM], BF16)
+        wo_sb = keep.tile([P, WO_BLOCKS, CHANNELS], BF16)
+        for u in range(UNITS):
+            w, hb = divmod(u, H_BLOCKS)
+            nc.sync.dma_start(out=x_sb[:, u, :], in_=x_dram[w, hb])
+            if hb == 0:
+                nc.sync.dma_start(out=kv_sb[:, w], in_=kv_dram[w])
+            if u == 0:
+                nc.sync.dma_start(out=bias_rows[0:1, :], in_=bo.rearrange("(o c) -> o c", o=1))
+            if u < WO_BLOCKS:
+                nc.sync.dma_start(out=wo_sb[:, u, :], in_=wo_dram[:, u, :])
+
         bias = keep.tile([P, OUT_CH], F32)
-        for ch in range(COL_HALVES):
-            cols = slice(ch * N_TILE, (ch + 1) * N_TILE)
-            spread = psum_y.tile([P, N_TILE], F32, tag="y_ps")
-            nc.tensor.matmul(out=spread[:], lhsT=ones[:], rhs=bias_rows[:, cols], start=True, stop=True)
-            nc.vector.tensor_copy(out=bias[:, cols], in_=spread[:])
+
+        def spread_bias():
+            for ch in range(COL_HALVES):
+                cols = slice(ch * N_TILE, (ch + 1) * N_TILE)
+                spread = psum_y.tile([P, N_TILE], F32, tag="y_ps")
+                nc.tensor.matmul(out=spread[:], lhsT=ones[:], rhs=bias_rows[:, cols], start=True, stop=True)
+                nc.vector.tensor_copy(out=bias[:, cols], in_=spread[:])
 
         wo_grouped = keep.tile([P, PASSES, OUT_CH, PACK], BF16, align_bytes=64)
         wo_codes = keep.tile([P, PASSES, OUT_CH], U32, align_bytes=64)
@@ -84,8 +89,8 @@ def tile_linear_retention_pb_kernel(tc, ret_w, kv_h, Wo, bo, out):
                 in_=wo_t[:].rearrange("p (g t) c -> p g c t", t=PACK),
             )
 
-        def quantise_wo(j):
-            cols = slice(j * WO_COLS, (j + 1) * WO_COLS)
+        def quantise_wo_block(cb):
+            cols = slice(cb * P, (cb + 1) * P)
             for g in range(PASSES):
                 nc.vector.quantize_mx(
                     out=wo_codes[:, g, cols].bitcast(FP8X4),
@@ -109,7 +114,7 @@ def tile_linear_retention_pb_kernel(tc, ret_w, kv_h, Wo, bo, out):
             x_t[u] = x_t_sb
 
         def read_out(u):
-            w = u % WIDTH
+            w = u // H_BLOCKS
             grouped = work.tile([P, PASSES, P, PACK], BF16, tag="o_grouped", align_bytes=64)
             for g in range(PASSES):
                 o_ps = psum_o.tile([P, PACK, P], F32, tag="o_ps")
@@ -117,7 +122,7 @@ def tile_linear_retention_pb_kernel(tc, ret_w, kv_h, Wo, bo, out):
                     n = g * PACK + t
                     nc.tensor.matmul(
                         out=o_ps[:, t, :],
-                        lhsT=kv_sb[:, w * HEADS + n, :],
+                        lhsT=kv_sb[:, w, n, :],
                         rhs=x_t[u][:, n, :],
                         start=True,
                         stop=True,
@@ -137,6 +142,7 @@ def tile_linear_retention_pb_kernel(tc, ret_w, kv_h, Wo, bo, out):
             o_scales[u] = scales
 
         def project(u):
+            w, hb = divmod(u, H_BLOCKS)
             for ch in range(COL_HALVES):
                 cols = slice(ch * N_TILE, (ch + 1) * N_TILE)
                 y_ps = psum_y.tile([P, N_TILE], F32, tag="y_ps")
@@ -152,19 +158,21 @@ def tile_linear_retention_pb_kernel(tc, ret_w, kv_h, Wo, bo, out):
                     )
                 y = results.tile([P, N_TILE], F32, tag="y")
                 nc.vector.tensor_tensor(out=y[:], in0=y_ps[:], in1=bias[:, cols], op=mybir.AluOpType.add)
-                nc.sync.dma_start(out=out_dram[u // WIDTH, u % WIDTH][:, cols], in_=y[:])
+                nc.sync.dma_start(out=out_dram[w, hb][:, cols], in_=y[:])
 
-        for i in range(UNITS + MX_LAG):
-            if i < WO_ROUNDS:
-                for cb in range(i * WO_PER_ROUND, (i + 1) * WO_PER_ROUND):
-                    transpose_wo_block(cb)
-            if i < UNITS:
-                transpose_unit(i)
-            if 0 <= i - 1 < UNITS:
-                read_out(i - 1)
+        for i in range(ROUNDS):
             if 0 <= i - 2 < UNITS:
                 quantise_unit(i - 2)
-            if 0 <= i - 1 < WO_ROUNDS:
-                quantise_wo(i - 1)
-            if 0 <= i - MX_LAG:
-                project(i - MX_LAG)
+            if 0 <= i - 2 < WO_BLOCKS:
+                quantise_wo_block(i - 2)
+            if i < UNITS:
+                transpose_unit(i)
+            if i == 0:
+                spread_bias()
+            if 0 <= i - 1 < WO_BLOCKS:
+                transpose_wo_block(i - 1)
+            if 0 <= i - 1 < UNITS:
+                read_out(i - 1)
+            if i >= MX_FIRST:
+                for u in range((i - MX_FIRST) * MX_UNITS, (i - MX_FIRST + 1) * MX_UNITS):
+                    project(u)

@@ -113,22 +113,22 @@ def tile_linear_retention_pb_kernel(tc, ret_w, kv_h, Wo, bo, out):
             nc.scalar.copy(out=x_t_sb[:], in_=x_t_ps[:])
             x_t[u] = x_t_sb
 
-        def read_out(u):
+        def read_out(u, g):
             w = u // H_BLOCKS
-            grouped = work.tile([P, PASSES, P, PACK], BF16, tag="o_grouped", align_bytes=64)
-            for g in range(PASSES):
-                o_ps = psum_o.tile([P, PACK, P], F32, tag="o_ps")
-                for t in range(PACK):
-                    n = g * PACK + t
-                    nc.tensor.matmul(
-                        out=o_ps[:, t, :],
-                        lhsT=kv_sb[:, w, n, :],
-                        rhs=x_t[u][:, n, :],
-                        start=True,
-                        stop=True,
-                    )
-                nc.scalar.copy(out=grouped[:, g], in_=o_ps[:].rearrange("p t h -> p h t"))
-            o_grouped[u] = grouped
+            if g == 0:
+                grouped = work.tile([P, PASSES, P, PACK], BF16, tag="o_grouped", align_bytes=64)
+                o_grouped[u] = grouped
+            o_ps = psum_o.tile([P, PACK, P], F32, tag="o_ps")
+            for t in range(PACK):
+                n = g * PACK + t
+                nc.tensor.matmul(
+                    out=o_ps[:, t, :],
+                    lhsT=kv_sb[:, w, n, :],
+                    rhs=x_t[u][:, n, :],
+                    start=True,
+                    stop=True,
+                )
+            nc.scalar.copy(out=o_grouped[u][:, g], in_=o_ps[:].rearrange("p t h -> p h t"))
 
         def quantise_unit(u):
             codes = quantised.tile([P, PASSES, P], U32, tag="o_codes", align_bytes=64)
@@ -165,6 +165,8 @@ def tile_linear_retention_pb_kernel(tc, ret_w, kv_h, Wo, bo, out):
                 quantise_unit(i - 2)
             if 0 <= i - 2 < WO_BLOCKS:
                 quantise_wo_block(i - 2)
+            if 0 <= i - 1 < UNITS:
+                read_out(i - 1, 0)
             if i < UNITS:
                 transpose_unit(i)
             if i == 0:
@@ -172,7 +174,7 @@ def tile_linear_retention_pb_kernel(tc, ret_w, kv_h, Wo, bo, out):
             if 0 <= i - 1 < WO_BLOCKS:
                 transpose_wo_block(i - 1)
             if 0 <= i - 1 < UNITS:
-                read_out(i - 1)
+                read_out(i - 1, 1)
             if i >= MX_FIRST:
                 for u in range((i - MX_FIRST) * MX_UNITS, (i - MX_FIRST + 1) * MX_UNITS):
                     project(u)

@@ -20,6 +20,7 @@ N_TILE = 512
 COL_HALVES = OUT_CH // N_TILE
 WO_BLOCKS = OUT_CH // P
 MX_UNITS = 2
+WARM_UP = 5
 ROUNDS = UNITS + 2
 MX_FIRST = ROUNDS - UNITS // MX_UNITS
 assert MX_FIRST > WO_BLOCKS + 1
@@ -45,12 +46,16 @@ def tile_linear_retention_pb_kernel(tc, ret_w, kv_h, Wo, bo, out):
         psum_y = ctx.enter_context(tc.psum_pool(name="psum_y", bufs=MX_UNITS * COL_HALVES))
         ctx.enter_context(tc.manual_schedule())
 
+        ones = keep.tile([P, N_TILE], BF16)
+        nc.vector.memset(ones[:], 1.0)
         bias_rows = keep.tile([P, OUT_CH], BF16)
         nc.vector.memset(bias_rows[:], 0.0)
-        ones = keep.tile([P, P], BF16)
-        nc.vector.memset(ones[:], 1.0)
         ident = keep.tile([P, P], BF16)
         make_identity(nc, ident[:])
+
+        warm = psum_y.tile([P, N_TILE], F32, tag="y_ps")
+        for repeat in range(WARM_UP):
+            nc.tensor.matmul(out=warm[:], lhsT=ones[:, :P], rhs=ones[:], start=True, stop=True)
 
         x_sb = keep.tile([P, UNITS, CHANNELS], BF16)
         kv_sb = keep.tile([P, WIDTH, HEADS, HEAD_DIM], BF16)
@@ -71,7 +76,7 @@ def tile_linear_retention_pb_kernel(tc, ret_w, kv_h, Wo, bo, out):
             for ch in range(COL_HALVES):
                 cols = slice(ch * N_TILE, (ch + 1) * N_TILE)
                 spread = psum_y.tile([P, N_TILE], F32, tag="y_ps")
-                nc.tensor.matmul(out=spread[:], lhsT=ones[:], rhs=bias_rows[:, cols], start=True, stop=True)
+                nc.tensor.matmul(out=spread[:], lhsT=ones[:, :P], rhs=bias_rows[:, cols], start=True, stop=True)
                 nc.vector.tensor_copy(out=bias[:, cols], in_=spread[:])
 
         wo_grouped = keep.tile([P, PASSES, OUT_CH, PACK], BF16, align_bytes=64)

@@ -19,11 +19,8 @@ UNITS = WIDTH * H_BLOCKS
 N_TILE = 512
 COL_HALVES = OUT_CH // N_TILE
 WO_BLOCKS = OUT_CH // P
-MX_UNITS = 2
-WARM_UP = 5
-ROUNDS = UNITS + 2
-MX_FIRST = ROUNDS - UNITS // MX_UNITS
-assert MX_FIRST > WO_BLOCKS + 1
+HALF_BLOCKS = N_TILE // P
+MX_LAG = COL_HALVES + 1
 
 FLOPS = 2 * HEIGHT * WIDTH * CHANNELS * HEAD_DIM + 2 * HEIGHT * WIDTH * CHANNELS * OUT_CH
 
@@ -39,23 +36,19 @@ def tile_linear_retention_pb_kernel(tc, ret_w, kv_h, Wo, bo, out):
     with ExitStack() as ctx:
         keep = ctx.enter_context(tc.tile_pool(name="keep", bufs=1))
         work = ctx.enter_context(tc.tile_pool(name="work", bufs=3))
-        quantised = ctx.enter_context(tc.tile_pool(name="quantised", bufs=MX_FIRST))
+        quantised = ctx.enter_context(tc.tile_pool(name="quantised", bufs=3))
         results = ctx.enter_context(tc.tile_pool(name="results", bufs=8))
-        psum_t = ctx.enter_context(tc.psum_pool(name="psum_t", bufs=2))
+        psum_t = ctx.enter_context(tc.psum_pool(name="psum_t", bufs=4))
         psum_o = ctx.enter_context(tc.psum_pool(name="psum_o", bufs=PASSES))
-        psum_y = ctx.enter_context(tc.psum_pool(name="psum_y", bufs=MX_UNITS * COL_HALVES))
+        psum_y = ctx.enter_context(tc.psum_pool(name="psum_y", bufs=COL_HALVES))
         ctx.enter_context(tc.manual_schedule())
 
-        ones = keep.tile([P, N_TILE], BF16)
-        nc.vector.memset(ones[:], 1.0)
         bias_rows = keep.tile([P, OUT_CH], BF16)
         nc.vector.memset(bias_rows[:], 0.0)
+        ones = keep.tile([P, P], BF16)
+        nc.vector.memset(ones[:], 1.0)
         ident = keep.tile([P, P], BF16)
         make_identity(nc, ident[:])
-
-        warm = psum_y.tile([P, N_TILE], F32, tag="y_ps")
-        for repeat in range(WARM_UP):
-            nc.tensor.matmul(out=warm[:], lhsT=ones[:, :P], rhs=ones[:], start=True, stop=True)
 
         x_sb = keep.tile([P, UNITS, CHANNELS], BF16)
         kv_sb = keep.tile([P, WIDTH, HEADS, HEAD_DIM], BF16)
@@ -67,8 +60,9 @@ def tile_linear_retention_pb_kernel(tc, ret_w, kv_h, Wo, bo, out):
                 nc.sync.dma_start(out=kv_sb[:, w], in_=kv_dram[w])
             if u == 0:
                 nc.sync.dma_start(out=bias_rows[0:1, :], in_=bo.rearrange("(o c) -> o c", o=1))
-            if u < WO_BLOCKS:
-                nc.sync.dma_start(out=wo_sb[:, u, :], in_=wo_dram[:, u, :])
+            if 0 <= u - 1 < COL_HALVES:
+                for cb in range((u - 1) * HALF_BLOCKS, u * HALF_BLOCKS):
+                    nc.sync.dma_start(out=wo_sb[:, cb, :], in_=wo_dram[:, cb, :])
 
         bias = keep.tile([P, OUT_CH], F32)
 
@@ -76,7 +70,7 @@ def tile_linear_retention_pb_kernel(tc, ret_w, kv_h, Wo, bo, out):
             for ch in range(COL_HALVES):
                 cols = slice(ch * N_TILE, (ch + 1) * N_TILE)
                 spread = psum_y.tile([P, N_TILE], F32, tag="y_ps")
-                nc.tensor.matmul(out=spread[:], lhsT=ones[:, :P], rhs=bias_rows[:, cols], start=True, stop=True)
+                nc.tensor.matmul(out=spread[:], lhsT=ones[:], rhs=bias_rows[:, cols], start=True, stop=True)
                 nc.vector.tensor_copy(out=bias[:, cols], in_=spread[:])
 
         wo_grouped = keep.tile([P, PASSES, OUT_CH, PACK], BF16, align_bytes=64)
@@ -89,13 +83,15 @@ def tile_linear_retention_pb_kernel(tc, ret_w, kv_h, Wo, bo, out):
                 nc.tensor.transpose(
                     out=wo_t[:, n, :], in_=wo_sb[:, cb, n * P : (n + 1) * P], identity=ident[:]
                 )
-            nc.vector.tensor_copy(
-                out=wo_grouped[:, :, cb * P : (cb + 1) * P, :],
-                in_=wo_t[:].rearrange("p (g t) c -> p g c t", t=PACK),
-            )
+            grouped_block = wo_grouped[:, :, cb * P : (cb + 1) * P, :]
+            hopping = wo_t[:].rearrange("p (g t) c -> p g c t", t=PACK)
+            if cb % 2 == 0:
+                nc.vector.tensor_copy(out=grouped_block, in_=hopping)
+            else:
+                nc.scalar.copy(out=grouped_block, in_=hopping)
 
-        def quantise_wo_block(cb):
-            cols = slice(cb * P, (cb + 1) * P)
+        def quantise_wo_half(ch):
+            cols = slice(ch * N_TILE, (ch + 1) * N_TILE)
             for g in range(PASSES):
                 nc.vector.quantize_mx(
                     out=wo_codes[:, g, cols].bitcast(FP8X4),
@@ -165,21 +161,21 @@ def tile_linear_retention_pb_kernel(tc, ret_w, kv_h, Wo, bo, out):
                 nc.vector.tensor_tensor(out=y[:], in0=y_ps[:], in1=bias[:, cols], op=mybir.AluOpType.add)
                 nc.sync.dma_start(out=out_dram[w, hb][:, cols], in_=y[:])
 
-        for i in range(ROUNDS):
+        for i in range(UNITS + MX_LAG):
             if 0 <= i - 2 < UNITS:
                 quantise_unit(i - 2)
-            if 0 <= i - 2 < WO_BLOCKS:
-                quantise_wo_block(i - 2)
+            if 0 <= i - 2 < COL_HALVES:
+                quantise_wo_half(i - 2)
             if 0 <= i - 1 < UNITS:
                 read_out(i - 1, 0)
             if i < UNITS:
                 transpose_unit(i)
             if i == 0:
                 spread_bias()
-            if 0 <= i - 1 < WO_BLOCKS:
-                transpose_wo_block(i - 1)
+            if 0 <= i - 1 < COL_HALVES:
+                for cb in range((i - 1) * HALF_BLOCKS, i * HALF_BLOCKS):
+                    transpose_wo_block(cb)
             if 0 <= i - 1 < UNITS:
                 read_out(i - 1, 1)
-            if i >= MX_FIRST:
-                for u in range((i - MX_FIRST) * MX_UNITS, (i - MX_FIRST + 1) * MX_UNITS):
-                    project(u)
+            if i >= MX_LAG:
+                project(i - MX_LAG)

from contextlib import ExitStack

import concourse.mybir as mybir
from concourse.masks import make_identity

BF16 = mybir.dt.bfloat16
F32 = mybir.dt.float32
U32 = mybir.dt.uint32
U8 = mybir.dt.uint8
FP8X4 = mybir.dt.float8_e4m3fn_x4

P = 128
HEIGHT, WIDTH, HEADS, HEAD_DIM, OUT_CH = 512, 4, 8, 128, 1024
CHANNELS = HEADS * HEAD_DIM
PACK = 4
PASSES = CHANNELS // (P * PACK)
H_BLOCKS = HEIGHT // P
UNITS = WIDTH * H_BLOCKS
N_TILE = 512
COL_HALVES = OUT_CH // N_TILE
WO_BLOCKS = OUT_CH // P
HALF_BLOCKS = N_TILE // P
MX_LAG = COL_HALVES + 1

FLOPS = 2 * HEIGHT * WIDTH * CHANNELS * HEAD_DIM + 2 * HEIGHT * WIDTH * CHANNELS * OUT_CH


def tile_linear_retention_pb_kernel(tc, ret_w, kv_h, Wo, bo, out):
    nc = tc.nc

    x_dram = ret_w[0].rearrange("(hb h) w n e -> w hb h (n e)", h=P)
    kv_dram = kv_h[0].rearrange("w n e f -> w e n f")
    wo_dram = Wo.rearrange("(cb c) k -> c cb k", c=P)
    out_dram = out[0].rearrange("(hb h w) c -> w hb h c", h=P, w=WIDTH)

    with ExitStack() as ctx:
        keep = ctx.enter_context(tc.tile_pool(name="keep", bufs=1))
        work = ctx.enter_context(tc.tile_pool(name="work", bufs=3))
        quantised = ctx.enter_context(tc.tile_pool(name="quantised", bufs=3))
        results = ctx.enter_context(tc.tile_pool(name="results", bufs=8))
        psum_t = ctx.enter_context(tc.psum_pool(name="psum_t", bufs=4))
        psum_o = ctx.enter_context(tc.psum_pool(name="psum_o", bufs=PASSES))
        psum_y = ctx.enter_context(tc.psum_pool(name="psum_y", bufs=COL_HALVES))
        ctx.enter_context(tc.manual_schedule())

        bias_rows = keep.tile([P, OUT_CH], BF16)
        nc.vector.memset(bias_rows[:], 0.0)
        ones = keep.tile([P, P], BF16)
        nc.vector.memset(ones[:], 1.0)
        ident = keep.tile([P, P], BF16)
        make_identity(nc, ident[:])

        x_sb = keep.tile([P, UNITS, CHANNELS], BF16)
        kv_sb = keep.tile([P, WIDTH, HEADS, HEAD_DIM], BF16)
        wo_sb = keep.tile([P, WO_BLOCKS, CHANNELS], BF16)
        for u in range(UNITS):
            w, hb = divmod(u, H_BLOCKS)
            nc.sync.dma_start(out=x_sb[:, u, :], in_=x_dram[w, hb])
            if hb == 0:
                nc.sync.dma_start(out=kv_sb[:, w], in_=kv_dram[w])
            if u == 0:
                nc.sync.dma_start(out=bias_rows[0:1, :], in_=bo.rearrange("(o c) -> o c", o=1))
            if 0 <= u - 1 < COL_HALVES:
                for cb in range((u - 1) * HALF_BLOCKS, u * HALF_BLOCKS):
                    nc.sync.dma_start(out=wo_sb[:, cb, :], in_=wo_dram[:, cb, :])

        bias = keep.tile([P, OUT_CH], F32)

        def spread_bias():
            for ch in range(COL_HALVES):
                cols = slice(ch * N_TILE, (ch + 1) * N_TILE)
                spread = psum_y.tile([P, N_TILE], F32, tag="y_ps")
                nc.tensor.matmul(out=spread[:], lhsT=ones[:], rhs=bias_rows[:, cols], start=True, stop=True)
                nc.vector.tensor_copy(out=bias[:, cols], in_=spread[:])

        wo_grouped = keep.tile([P, PASSES, OUT_CH, PACK], BF16, align_bytes=64)
        wo_codes = keep.tile([P, PASSES, OUT_CH], U32, align_bytes=64)
        wo_scales = keep.tile([P, PASSES, OUT_CH], U8, align_bytes=64)

        def transpose_wo_block(cb):
            wo_t = psum_t.tile([P, HEADS, P], BF16, tag="t_ps")
            for n in range(HEADS):
                nc.tensor.transpose(
                    out=wo_t[:, n, :], in_=wo_sb[:, cb, n * P : (n + 1) * P], identity=ident[:]
                )
            grouped_block = wo_grouped[:, :, cb * P : (cb + 1) * P, :]
            hopping = wo_t[:].rearrange("p (g t) c -> p g c t", t=PACK)
            if cb % 2 == 0:
                nc.vector.tensor_copy(out=grouped_block, in_=hopping)
            else:
                nc.scalar.copy(out=grouped_block, in_=hopping)

        def quantise_wo_half(ch):
            cols = slice(ch * N_TILE, (ch + 1) * N_TILE)
            for g in range(PASSES):
                nc.vector.quantize_mx(
                    out=wo_codes[:, g, cols].bitcast(FP8X4),
                    scales=wo_scales[:, g, cols],
                    in_=wo_grouped[:, g, cols, :].rearrange("p c t -> p (c t)"),
                )

        x_t = {}
        o_grouped = {}
        o_codes = {}
        o_scales = {}

        def transpose_unit(u):
            x_t_ps = psum_t.tile([P, HEADS, P], BF16, tag="t_ps")
            for n in range(HEADS):
                nc.tensor.transpose(
                    out=x_t_ps[:, n, :], in_=x_sb[:, u, n * P : (n + 1) * P], identity=ident[:]
                )
            x_t_sb = work.tile([P, HEADS, P], BF16, tag="x_t")
            nc.scalar.copy(out=x_t_sb[:], in_=x_t_ps[:])
            x_t[u] = x_t_sb

        def read_out(u, g):
            w = u // H_BLOCKS
            if g == 0:
                grouped = work.tile([P, PASSES, P, PACK], BF16, tag="o_grouped", align_bytes=64)
                o_grouped[u] = grouped
            o_ps = psum_o.tile([P, PACK, P], F32, tag="o_ps")
            for t in range(PACK):
                n = g * PACK + t
                nc.tensor.matmul(
                    out=o_ps[:, t, :],
                    lhsT=kv_sb[:, w, n, :],
                    rhs=x_t[u][:, n, :],
                    start=True,
                    stop=True,
                )
            nc.scalar.copy(out=o_grouped[u][:, g], in_=o_ps[:].rearrange("p t h -> p h t"))

        def quantise_unit(u):
            codes = quantised.tile([P, PASSES, P], U32, tag="o_codes", align_bytes=64)
            scales = quantised.tile([P, PASSES, P], U8, tag="o_scales", align_bytes=64)
            nc.vector.quantize_mx(
                out=codes[:].rearrange("p g h -> p (g h)").bitcast(FP8X4),
                scales=scales[:].rearrange("p g h -> p (g h)"),
                in_=o_grouped[u][:].rearrange("p g h t -> p (g h t)"),
            )
            o_codes[u] = codes
            o_scales[u] = scales

        def project(u):
            w, hb = divmod(u, H_BLOCKS)
            for ch in range(COL_HALVES):
                cols = slice(ch * N_TILE, (ch + 1) * N_TILE)
                y_ps = psum_y.tile([P, N_TILE], F32, tag="y_ps")
                for g in range(PASSES):
                    nc.tensor.matmul_mx(
                        out=y_ps[:],
                        lhsT=o_codes[u][:, g, :].bitcast(FP8X4),
                        lhsT_scale=o_scales[u][:, g, :],
                        rhs=wo_codes[:, g, cols].bitcast(FP8X4),
                        rhs_scale=wo_scales[:, g, cols],
                        start=(g == 0),
                        stop=(g == PASSES - 1),
                    )
                y = results.tile([P, N_TILE], F32, tag="y")
                nc.vector.tensor_tensor(out=y[:], in0=y_ps[:], in1=bias[:, cols], op=mybir.AluOpType.add)
                nc.sync.dma_start(out=out_dram[w, hb][:, cols], in_=y[:])

        for i in range(UNITS + MX_LAG):
            if 0 <= i - 2 < UNITS:
                quantise_unit(i - 2)
            if 0 <= i - 2 < COL_HALVES:
                quantise_wo_half(i - 2)
            if 0 <= i - 1 < UNITS:
                read_out(i - 1, 0)
            if i < UNITS:
                transpose_unit(i)
            if i == 0:
                spread_bias()
            if 0 <= i - 1 < COL_HALVES:
                for cb in range((i - 1) * HALF_BLOCKS, i * HALF_BLOCKS):
                    transpose_wo_block(cb)
            if 0 <= i - 1 < UNITS:
                read_out(i - 1, 1)
            if i >= MX_LAG:
                project(i - MX_LAG)
